import numpy as np
import ml_dtypes


def mxq(x, axis, fmt="e4m3"):
    dtype, down = {"e4m3": (ml_dtypes.float8_e4m3fn, 7), "e5m2": (ml_dtypes.float8_e5m2, 14)}[fmt]
    v = np.moveaxis(np.asarray(x, np.float32).astype(ml_dtypes.bfloat16).astype(np.float64), axis, -1)
    blocks = v.reshape(v.shape[:-1] + (-1, 32))
    amax = np.abs(blocks).max(-1, keepdims=True)
    byte = np.maximum(np.where(amax > 0, np.frexp(amax)[1] - 1 + 127, 0) - down, 1)
    scale = np.exp2(byte - 127.0)
    codes = (blocks / scale).astype(np.float32).astype(dtype).astype(np.float64)
    return np.moveaxis((codes * scale).reshape(v.shape), -1, axis)


WIDE = False


def mx_kscale(k):
    if not WIDE:
        return np.ones(k)
    levels = np.array([10, -10, 5, -5, 0])
    a = np.random.permutation(np.resize(levels, k // 512 * 4)).reshape(k // 512, 4)
    idx = np.arange(k)
    return np.exp2(a[idx // 512, idx % 128 // 32])


BF16 = ml_dtypes.bfloat16


def bf(x):
    return np.asarray(x, np.float32).astype(BF16)


def f64(x):
    return np.asarray(x).astype(np.float64)


B, L, D, H, HD, FF = 4, 1024, 1024, 2, 128, 4096
EPS = 1e-6
DA = H * HD


def rmsnorm(x, w):
    return x * (1.0 / np.sqrt(np.mean(x * x, axis=-1, keepdims=True) + EPS)) * w


def setup_inputs():
    s = mx_kscale(D)
    return {"x": bf(np.random.standard_normal((B, L, D))),
            "norm1_w": bf((1.0 + 0.1 * np.random.standard_normal(D)) * s),
            "qkv_w": bf(np.random.standard_normal((3 * DA, D)) / np.sqrt(D) / s[None, :])}


def reference(x, norm1_w, qkv_w):
    h = rmsnorm(f64(x), f64(norm1_w))
    qkv = mxq(h, 2, "e4m3") @ mxq(f64(qkv_w), 1, "e4m3").T
    qkv = qkv.reshape(B, L, 3, H, HD)
    q, k, v = (np.moveaxis(qkv, 2, 0)[i].transpose(0, 2, 1, 3) for i in range(3))
    return q, k, v

@@ -1,0 +1,336 @@
+from contextlib import ExitStack
+
+import concourse.mybir as mybir
+from concourse.masks import make_identity
+
+BF16 = mybir.dt.bfloat16
+F32 = mybir.dt.float32
+U32 = mybir.dt.uint32
+U8 = mybir.dt.uint8
+FP8X4 = mybir.dt.float8_e4m3fn_x4
+ACT = mybir.ActivationFunctionType
+ALU = mybir.AluOpType
+
+P = 128
+NB = 4
+L = 1024
+D = 1024
+NOUT = 768
+JB = L // P
+NT = NB * JB
+EPS = 1e-6
+FLOPS = 2 * NB * L * D * NOUT
+
+MANUAL = True
+G_FROM = 4
+FB_V_UNTIL = 24
+LA = 6
+LI = 3
+LC = 2
+LM = 2
+LF = 3
+PROLOGUE = (
+    ("A", 0, "x"),
+    ("R", 0, "x"),
+    ("I", 0, "x"),
+    ("GP", 0, "x"),
+    ("C", 0, "v"),
+    ("T", 0, "x"),
+    ("A", 1, "x"),
+    ("R", 1, "x"),
+    ("I", 1, "x"),
+    ("C", 1, "v"),
+    ("D", 0, "x"),
+    ("T", 1, "x"),
+    ("A", 2, "x"),
+    ("A", 3, "x"),
+    ("R", 2, "x"),
+    ("WT", 0, "x"),
+    ("WT", 1, "x"),
+    ("WC", 0, "s"),
+    ("WC", 1, "s"),
+    ("D", 1, "x"),
+    ("I", 2, "x"),
+    ("C", 2, "v"),
+    ("C", 3, "v"),
+    ("WT", 2, "x"),
+    ("WT", 3, "x"),
+    ("WC", 2, "v"),
+    ("WC", 3, "s"),
+    ("WT", 4, "x"),
+    ("WT", 5, "x"),
+    ("WC", 4, "v"),
+    ("WC", 5, "s"),
+    ("WQ", 0, "x"),
+    ("WQ", 1, "x"),
+)
+
+
+def tile_transformerblock_pa_t_kernel(tc, x, norm1_w, qkv_w, out_0, out_1, out_2):
+    nc = tc.nc
+    outs = (out_0, out_1, out_2)
+    xf = x.flatten_outer_dims()
+
+    groups = [(0, 1), (1, 2)] + [(s, s + 2) for s in range(2, NT, 2)]
+    group_of = {}
+    for gi, (s, e) in enumerate(groups):
+        for t in range(s, e):
+            group_of[t] = gi
+    loads = [(0, 0, 1), (0, 1, 2), (0, 2, 4), (0, 4, 8)]
+    loads += [(b, j, j + 4) for b in range(1, NB) for j in (0, 4)]
+    stores = [(b, j, j + 4) for b in range(NB - 1) for j in (0, 4)]
+    stores += [(NB - 1, 0, 2), (NB - 1, 2, 4), (NB - 1, 4, 6), (NB - 1, 6, 7), (NB - 1, 7, 8)]
+    load_of = {}
+    for li, (b, j0, j1) in enumerate(loads):
+        for j in range(j0, j1):
+            load_of[b * JB + j] = li
+    store_of = {}
+    for si, (b, j0, j1) in enumerate(stores):
+        for j in range(j0, j1):
+            store_of[b * JB + j] = si
+
+    with ExitStack() as ctx:
+        const = ctx.enter_context(tc.tile_pool(name="const", bufs=1))
+        xsp = ctx.enter_context(tc.tile_pool(name="xsp", bufs=6))
+        grp = ctx.enter_context(tc.tile_pool(name="grp", bufs=3))
+        cdp = ctx.enter_context(tc.tile_pool(name="cdp", bufs=3))
+        jkp = ctx.enter_context(tc.tile_pool(name="jkp", bufs=2))
+        osp = ctx.enter_context(tc.tile_pool(name="osp", bufs=4))
+        ps_t = ctx.enter_context(tc.psum_pool(name="ps_t", bufs=4))
+        ps_a = ctx.enter_context(tc.psum_pool(name="ps_a", bufs=2))
+        ps_b = ctx.enter_context(tc.psum_pool(name="ps_b", bufs=2))
+        if MANUAL:
+            ctx.enter_context(tc.manual_schedule())
+
+        idf = const.tile([P, P], F32, name="idf")
+        idb = const.tile([P, P], BF16, name="idb")
+        gt = const.tile([P, P], BF16, name="gt")
+        g32 = const.tile([P, 8], F32, name="g32")
+        epst = const.tile([P, 1], F32, name="epst")
+        warm = const.tile([P, 1], F32, name="warm")
+        wsb = const.tile([P, 6, D], BF16, name="wsb")
+        wg = const.tile([P, 2, NOUT, 4], BF16, name="wg", align_bytes=64)
+        wc = const.tile([P, 2, NOUT], U32, name="wc", align_bytes=64)
+        ws = const.tile([P, 2, NOUT], U8, name="ws", align_bytes=64)
+        xt = [const.tile([P, j1 - j0, D], BF16, name="xt%d" % li) for li, (b, j0, j1) in enumerate(loads)]
+        ms = [const.tile([P, e - s], F32, name="ms%d" % gi) for gi, (s, e) in enumerate(groups)]
+        sq = [const.tile([P, e - s], F32, name="sq%d" % gi) for gi, (s, e) in enumerate(groups)]
+        rs = [const.tile([P, e - s], F32, name="rs%d" % gi) for gi, (s, e) in enumerate(groups)]
+
+        nc.vector.memset(gt[:], 0.0)
+        nc.vector.memset(epst[:], EPS)
+        make_identity(nc, idb[:])
+        make_identity(nc, idf[:])
+        nc.scalar.dma_start(out=gt[0:8, :], in_=norm1_w.rearrange("(r c) -> r c", c=P))
+
+        def load_x(li):
+            b, j0, j1 = loads[li]
+            src = xf[b * L : (b + 1) * L, :].rearrange("(p j) d -> p j d", j=JB)
+            nc.sync.dma_start(out=xt[li][:], in_=src[:, j0:j1, :])
+
+        def load_w(a0, a1):
+            src = qkv_w.rearrange("(a p) k -> p a k", p=P)
+            nc.sync.dma_start(out=wsb[:, a0:a1, :], in_=src[:, a0:a1, :])
+
+        load_x(0)
+        load_x(1)
+        load_x(2)
+        load_w(0, 2)
+        load_w(2, 4)
+        load_w(4, 6)
+        for li in range(3, len(loads)):
+            load_x(li)
+
+        nc.scalar.activation(out=warm[:], in_=epst[:], func=ACT.Sqrt)
+
+        def x_of(t):
+            li = load_of[t]
+            return xt[li][:, t % JB - loads[li][1], :]
+
+        def col_of(tiles, t):
+            gi = group_of[t]
+            c = t - groups[gi][0]
+            return tiles[gi][:, c : c + 1]
+
+        def sum_squares(t):
+            junk = jkp.tile([P, D], BF16, name="junk")
+            nc.scalar.activation(
+                out=junk[:], in_=x_of(t), func=ACT.Square, scale=1.0 / 32.0, accum_out=col_of(ms, t)
+            )
+
+        def root(gi):
+            nc.scalar.activation(out=sq[gi][:], in_=ms[gi][:], func=ACT.Sqrt, bias=epst[:, 0:1])
+
+        def invert(gi):
+            nc.vector.reciprocal(out=rs[gi][:], in_=sq[gi][:])
+
+        xs_of = {}
+        tb_of = {}
+        gr_of = {}
+        cd_of = {}
+        o_of = {}
+        os_of = {}
+
+        def scale_rows(t, engine):
+            xs = xsp.tile([P, D], F32, name="xs")
+            xs_of[t] = xs
+            if engine == "g":
+                nc.gpsimd.tensor_scalar(
+                    out=xs[:], in0=x_of(t), scalar1=col_of(rs, t), scalar2=1.0, op0=ALU.mult, op1=ALU.mult
+                )
+            else:
+                nc.vector.tensor_scalar(out=xs[:], in0=x_of(t), scalar1=col_of(rs, t), scalar2=None, op0=ALU.mult)
+
+        def transposes(t):
+            xs = xs_of[t]
+            banks = []
+            for g in range(2):
+                tb = ps_t.tile([P, 4, P], F32, name="tb")
+                for u in range(4):
+                    c = 4 * g + u
+                    nc.tensor.transpose(out=tb[:, u, :], in_=xs[:, c * P : (c + 1) * P], identity=idf[:])
+                banks.append(tb)
+            tb_of[t] = banks
+
+        def gain_and_group(t):
+            if t % 2 == 0:
+                gr_of[t // 2] = grp.tile([P, 4, P, 4], BF16, name="gr", align_bytes=64)
+            gr = gr_of[t // 2]
+            for g in range(2):
+                nc.vector.tensor_tensor(
+                    out=gr[:, 2 * (t % 2) + g, :, :],
+                    in0=tb_of[t][g][:].rearrange("p u r -> p r u"),
+                    in1=g32[:, 4 * g : 4 * g + 4].unsqueeze(1).to_broadcast([P, P, 4]),
+                    op=ALU.mult,
+                )
+
+        def quantise(pair):
+            cd = cdp.tile([P, 4, P], U32, name="cd", align_bytes=64)
+            sc = cdp.tile([P, 4, P], U8, name="sc", align_bytes=64)
+            cd_of[pair] = (cd, sc)
+            nc.vector.quantize_mx(
+                out=cd[:].rearrange("p s r -> p (s r)").bitcast(FP8X4),
+                scales=sc[:].rearrange("p s r -> p (s r)"),
+                in_=gr_of[pair][:].rearrange("p s r u -> p (s r u)"),
+            )
+
+        def project(t):
+            cd, sc = cd_of[t // 2]
+            oa = ps_a.tile([P, 512], F32, name="oa")
+            ob = ps_b.tile([P, 256], F32, name="ob")
+            o_of[t] = (oa, ob)
+            for o, n0, n1 in ((oa, 0, 512), (ob, 512, NOUT)):
+                for g in range(2):
+                    s = 2 * (t % 2) + g
+                    nc.tensor.matmul_mx(
+                        out=o[:],
+                        lhsT=cd[:, s, :].bitcast(FP8X4),
+                        lhsT_scale=sc[:, s, :],
+                        rhs=wc[:, g, n0:n1].bitcast(FP8X4),
+                        rhs_scale=ws[:, g, n0:n1],
+                        start=(g == 0),
+                        stop=(g == 1),
+                    )
+
+        def results_out(t):
+            si = store_of[t]
+            b, j0, j1 = stores[si]
+            j = t % JB
+            if j == j0:
+                os_of[si] = osp.tile([P, 6, j1 - j0, P], F32, name="osb")
+            osb = os_of[si]
+            oa, ob = o_of[t]
+            nc.scalar.copy(out=osb[:, 0:4, j - j0, :], in_=oa[:].rearrange("p (c f) -> p c f", c=4))
+            if t < FB_V_UNTIL:
+                nc.vector.tensor_copy(out=osb[:, 4:6, j - j0, :], in_=ob[:].rearrange("p (c f) -> p c f", c=2))
+            else:
+                nc.scalar.copy(out=osb[:, 4:6, j - j0, :], in_=ob[:].rearrange("p (c f) -> p c f", c=2))
+            if j == j1 - 1:
+                for i in range(3):
+                    dst = outs[i].rearrange("b n l f -> (b n) l f")[2 * b : 2 * b + 2, :, :]
+                    dst = dst.rearrange("n (p j) f -> p n j f", j=JB)
+                    nc.sync.dma_start(out=dst[:, :, j0:j1, :], in_=osb[:, 2 * i : 2 * i + 2, :, :])
+
+        wp_of = {}
+
+        def w_transposes(a):
+            pool = ps_a if a % 4 < 2 else ps_b
+            wp = pool.tile([P, 8, P], BF16, name="wp", tag="oa" if a % 4 < 2 else "ob")
+            wp_of[a] = wp
+            for c in range(8):
+                nc.tensor.transpose(out=wp[:, c, :], in_=wsb[:, a, c * P : (c + 1) * P], identity=idb[:])
+
+        def w_group(a, engine):
+            dst = wg[:, :, a * P : (a + 1) * P, :]
+            src = wp_of[a][:].rearrange("p (g u) n -> p g n u", g=2)
+            if engine == "v":
+                nc.vector.tensor_copy(out=dst, in_=src)
+            else:
+                nc.scalar.copy(out=dst, in_=src)
+
+        def w_quantise(g, n0, n1):
+            nc.vector.quantize_mx(
+                out=wc[:, g, n0:n1].bitcast(FP8X4),
+                scales=ws[:, g, n0:n1],
+                in_=wg[:, g, n0:n1, :].rearrange("p n u -> p (n u)"),
+            )
+
+        def gain_columns():
+            gp = ps_t.tile([P, P], BF16, name="gp", tag="tb")
+            nc.tensor.transpose(out=gp[:], in_=gt[:], identity=idb[:])
+            nc.vector.tensor_copy(out=g32[:], in_=gp[:, 0:8])
+
+        done = set()
+        for kind, n, e in PROLOGUE:
+            done.add((kind, n))
+            if kind == "A":
+                sum_squares(n)
+            elif kind == "R":
+                root(n)
+            elif kind == "I":
+                invert(n)
+            elif kind == "C":
+                scale_rows(n, e)
+            elif kind == "T":
+                transposes(n)
+            elif kind == "D":
+                gain_and_group(n)
+            elif kind == "WT":
+                w_transposes(n)
+            elif kind == "WC":
+                w_group(n, e)
+            elif kind == "WQ":
+                for g in range(2):
+                    w_quantise(g, (0, 512)[n], (512, NOUT)[n])
+            elif kind == "GP":
+                gain_columns()
+            else:
+                assert False, kind
+
+        for it in range(-LA, NT + LF):
+            a = it + LA
+            if 0 <= a < NT:
+                if ("A", a) not in done:
+                    sum_squares(a)
+                if a == groups[group_of[a]][1] - 1 and ("R", group_of[a]) not in done:
+                    root(group_of[a])
+            if 0 <= it - LF < NT:
+                results_out(it - LF)
+            if 0 <= it < NT and ("D", it) not in done:
+                gain_and_group(it)
+            c = it + LC
+            if 0 <= c < min(NT, G_FROM) and ("C", c) not in done:
+                scale_rows(c, "v")
+            if 0 <= it + 1 < NT and ("T", it + 1) not in done:
+                transposes(it + 1)
+            if it % 2 == 1 and 1 <= it < NT:
+                quantise((it - 1) // 2)
+            r = it + LI
+            if 0 <= r < NT and r == groups[group_of[r]][0]:
+                if ("I", group_of[r]) not in done:
+                    invert(group_of[r])
+                for t in range(groups[group_of[r]][0], groups[group_of[r]][1]):
+                    if t >= G_FROM and ("C", t) not in done:
+                        scale_rows(t, "g")
+            if 0 <= it - LM < NT:
+                project(it - LM)

@@ -22,8 +22,8 @@ EPS = 1e-6
 FLOPS = 2 * NB * L * D * NOUT
 
 MANUAL = True
-G_FROM = 4
-FB_V_UNTIL = 24
+G_FROM = 32
+FB_V_UNTIL = 0
 LA = 6
 LI = 3
 LC = 2

@@ -18,52 +18,13 @@ D = 1024
 NOUT = 768
 JB = L // P
 NT = NB * JB
+NP = NT // 2
 EPS = 1e-6
 FLOPS = 2 * NB * L * D * NOUT
 
-MANUAL = True
-G_FROM = 32
-FB_V_UNTIL = 0
-LA = 6
-LI = 3
-LC = 2
-LM = 2
-LF = 3
-PROLOGUE = (
-    ("A", 0, "x"),
-    ("R", 0, "x"),
-    ("I", 0, "x"),
-    ("GP", 0, "x"),
-    ("C", 0, "v"),
-    ("T", 0, "x"),
-    ("A", 1, "x"),
-    ("R", 1, "x"),
-    ("I", 1, "x"),
-    ("C", 1, "v"),
-    ("D", 0, "x"),
-    ("T", 1, "x"),
-    ("A", 2, "x"),
-    ("A", 3, "x"),
-    ("R", 2, "x"),
-    ("WT", 0, "x"),
-    ("WT", 1, "x"),
-    ("WC", 0, "s"),
-    ("WC", 1, "s"),
-    ("D", 1, "x"),
-    ("I", 2, "x"),
-    ("C", 2, "v"),
-    ("C", 3, "v"),
-    ("WT", 2, "x"),
-    ("WT", 3, "x"),
-    ("WC", 2, "v"),
-    ("WC", 3, "s"),
-    ("WT", 4, "x"),
-    ("WT", 5, "x"),
-    ("WC", 4, "v"),
-    ("WC", 5, "s"),
-    ("WQ", 0, "x"),
-    ("WQ", 1, "x"),
-)
+PA = 3
+PI = 2
+FB_V_UNTIL = 24
 
 
 def tile_transformerblock_pa_t_kernel(tc, x, norm1_w, qkv_w, out_0, out_1, out_2):
@@ -71,11 +32,6 @@ def tile_transformerblock_pa_t_kernel(tc, x, norm1_w, qkv_w, out_0, out_1, out_2
     outs = (out_0, out_1, out_2)
     xf = x.flatten_outer_dims()
 
-    groups = [(0, 1), (1, 2)] + [(s, s + 2) for s in range(2, NT, 2)]
-    group_of = {}
-    for gi, (s, e) in enumerate(groups):
-        for t in range(s, e):
-            group_of[t] = gi
     loads = [(0, 0, 1), (0, 1, 2), (0, 2, 4), (0, 4, 8)]
     loads += [(b, j, j + 4) for b in range(1, NB) for j in (0, 4)]
     stores = [(b, j, j + 4) for b in range(NB - 1) for j in (0, 4)]
@@ -91,7 +47,7 @@ def tile_transformerblock_pa_t_kernel(tc, x, norm1_w, qkv_w, out_0, out_1, out_2
 
     with ExitStack() as ctx:
         const = ctx.enter_context(tc.tile_pool(name="const", bufs=1))
-        xsp = ctx.enter_context(tc.tile_pool(name="xsp", bufs=6))
+        xsp = ctx.enter_context(tc.tile_pool(name="xsp", bufs=8))
         grp = ctx.enter_context(tc.tile_pool(name="grp", bufs=3))
         cdp = ctx.enter_context(tc.tile_pool(name="cdp", bufs=3))
         jkp = ctx.enter_context(tc.tile_pool(name="jkp", bufs=2))
@@ -99,8 +55,7 @@ def tile_transformerblock_pa_t_kernel(tc, x, norm1_w, qkv_w, out_0, out_1, out_2
         ps_t = ctx.enter_context(tc.psum_pool(name="ps_t", bufs=4))
         ps_a = ctx.enter_context(tc.psum_pool(name="ps_a", bufs=2))
         ps_b = ctx.enter_context(tc.psum_pool(name="ps_b", bufs=2))
-        if MANUAL:
-            ctx.enter_context(tc.manual_schedule())
+        ctx.enter_context(tc.manual_schedule())
 
         idf = const.tile([P, P], F32, name="idf")
         idb = const.tile([P, P], BF16, name="idb")
@@ -113,9 +68,9 @@ def tile_transformerblock_pa_t_kernel(tc, x, norm1_w, qkv_w, out_0, out_1, out_2
         wc = const.tile([P, 2, NOUT], U32, name="wc", align_bytes=64)
         ws = const.tile([P, 2, NOUT], U8, name="ws", align_bytes=64)
         xt = [const.tile([P, j1 - j0, D], BF16, name="xt%d" % li) for li, (b, j0, j1) in enumerate(loads)]
-        ms = [const.tile([P, e - s], F32, name="ms%d" % gi) for gi, (s, e) in enumerate(groups)]
-        sq = [const.tile([P, e - s], F32, name="sq%d" % gi) for gi, (s, e) in enumerate(groups)]
-        rs = [const.tile([P, e - s], F32, name="rs%d" % gi) for gi, (s, e) in enumerate(groups)]
+        ms = [const.tile([P, 2], F32, name="ms%d" % i) for i in range(NP)]
+        sq = [const.tile([P, 2], F32, name="sq%d" % i) for i in range(NP)]
+        rs = [const.tile([P, 2], F32, name="rs%d" % i) for i in range(NP)]
 
         nc.vector.memset(gt[:], 0.0)
         nc.vector.memset(epst[:], EPS)
@@ -147,22 +102,21 @@ def tile_transformerblock_pa_t_kernel(tc, x, norm1_w, qkv_w, out_0, out_1, out_2
             li = load_of[t]
             return xt[li][:, t % JB - loads[li][1], :]
 
-        def col_of(tiles, t):
-            gi = group_of[t]
-            c = t - groups[gi][0]
-            return tiles[gi][:, c : c + 1]
-
         def sum_squares(t):
             junk = jkp.tile([P, D], BF16, name="junk")
             nc.scalar.activation(
-                out=junk[:], in_=x_of(t), func=ACT.Square, scale=1.0 / 32.0, accum_out=col_of(ms, t)
+                out=junk[:], in_=x_of(t), func=ACT.Square, scale=1.0 / 32.0, accum_out=ms[t // 2][:, t % 2 : t % 2 + 1]
             )
 
-        def root(gi):
-            nc.scalar.activation(out=sq[gi][:], in_=ms[gi][:], func=ACT.Sqrt, bias=epst[:, 0:1])
+        def root(t0, t1):
+            i = t0 // 2
+            nc.scalar.activation(
+                out=sq[i][:, t0 % 2 : t1 - 2 * i], in_=ms[i][:, t0 % 2 : t1 - 2 * i], func=ACT.Sqrt, bias=epst[:, 0:1]
+            )
 
-        def invert(gi):
-            nc.vector.reciprocal(out=rs[gi][:], in_=sq[gi][:])
+        def invert(t0, t1):
+            i = t0 // 2
+            nc.vector.reciprocal(out=rs[i][:, t0 % 2 : t1 - 2 * i], in_=sq[i][:, t0 % 2 : t1 - 2 * i])
 
         xs_of = {}
         tb_of = {}
@@ -174,12 +128,11 @@ def tile_transformerblock_pa_t_kernel(tc, x, norm1_w, qkv_w, out_0, out_1, out_2
         def scale_rows(t, engine):
             xs = xsp.tile([P, D], F32, name="xs")
             xs_of[t] = xs
+            r = rs[t // 2][:, t % 2 : t % 2 + 1]
             if engine == "g":
-                nc.gpsimd.tensor_scalar(
-                    out=xs[:], in0=x_of(t), scalar1=col_of(rs, t), scalar2=1.0, op0=ALU.mult, op1=ALU.mult
-                )
+                nc.gpsimd.tensor_scalar(out=xs[:], in0=x_of(t), scalar1=r, scalar2=1.0, op0=ALU.mult, op1=ALU.mult)
             else:
-                nc.vector.tensor_scalar(out=xs[:], in0=x_of(t), scalar1=col_of(rs, t), scalar2=None, op0=ALU.mult)
+                nc.vector.tensor_scalar(out=xs[:], in0=x_of(t), scalar1=r, scalar2=None, op0=ALU.mult)
 
         def transposes(t):
             xs = xs_of[t]
@@ -192,26 +145,26 @@ def tile_transformerblock_pa_t_kernel(tc, x, norm1_w, qkv_w, out_0, out_1, out_2
                 banks.append(tb)
             tb_of[t] = banks
 
-        def gain_and_group(t):
-            if t % 2 == 0:
+        def gain_and_group(t, g):
+            if t % 2 == 0 and g == 0:
                 gr_of[t // 2] = grp.tile([P, 4, P, 4], BF16, name="gr", align_bytes=64)
-            gr = gr_of[t // 2]
-            for g in range(2):
-                nc.vector.tensor_tensor(
-                    out=gr[:, 2 * (t % 2) + g, :, :],
-                    in0=tb_of[t][g][:].rearrange("p u r -> p r u"),
-                    in1=g32[:, 4 * g : 4 * g + 4].unsqueeze(1).to_broadcast([P, P, 4]),
-                    op=ALU.mult,
-                )
+            nc.vector.tensor_tensor(
+                out=gr_of[t // 2][:, 2 * (t % 2) + g, :, :],
+                in0=tb_of[t][g][:].rearrange("p u r -> p r u"),
+                in1=g32[:, 4 * g : 4 * g + 4].unsqueeze(1).to_broadcast([P, P, 4]),
+                op=ALU.mult,
+            )
 
-        def quantise(pair):
-            cd = cdp.tile([P, 4, P], U32, name="cd", align_bytes=64)
-            sc = cdp.tile([P, 4, P], U8, name="sc", align_bytes=64)
-            cd_of[pair] = (cd, sc)
+        def quantise(i, s0, s1):
+            if s0 == 0:
+                cd = cdp.tile([P, 4, P], U32, name="cd", align_bytes=64)
+                sc = cdp.tile([P, 4, P], U8, name="sc", align_bytes=64)
+                cd_of[i] = (cd, sc)
+            cd, sc = cd_of[i]
             nc.vector.quantize_mx(
-                out=cd[:].rearrange("p s r -> p (s r)").bitcast(FP8X4),
-                scales=sc[:].rearrange("p s r -> p (s r)"),
-                in_=gr_of[pair][:].rearrange("p s r u -> p (s r u)"),
+                out=cd[:, s0:s1, :].rearrange("p s r -> p (s r)").bitcast(FP8X4),
+                scales=sc[:, s0:s1, :].rearrange("p s r -> p (s r)"),
+                in_=gr_of[i][:, s0:s1, :, :].rearrange("p s r u -> p (s r u)"),
             )
 
         def project(t):
@@ -232,7 +185,7 @@ def tile_transformerblock_pa_t_kernel(tc, x, norm1_w, qkv_w, out_0, out_1, out_2
                         stop=(g == 1),
                     )
 
-        def results_out(t):
+        def results_out(t, engine_b):
             si = store_of[t]
             b, j0, j1 = stores[si]
             j = t % JB
@@ -241,7 +194,7 @@ def tile_transformerblock_pa_t_kernel(tc, x, norm1_w, qkv_w, out_0, out_1, out_2
             osb = os_of[si]
             oa, ob = o_of[t]
             nc.scalar.copy(out=osb[:, 0:4, j - j0, :], in_=oa[:].rearrange("p (c f) -> p c f", c=4))
-            if t < FB_V_UNTIL:
+            if engine_b == "v":
                 nc.vector.tensor_copy(out=osb[:, 4:6, j - j0, :], in_=ob[:].rearrange("p (c f) -> p c f", c=2))
             else:
                 nc.scalar.copy(out=osb[:, 4:6, j - j0, :], in_=ob[:].rearrange("p (c f) -> p c f", c=2))
@@ -268,69 +221,92 @@ def tile_transformerblock_pa_t_kernel(tc, x, norm1_w, qkv_w, out_0, out_1, out_2
             else:
                 nc.scalar.copy(out=dst, in_=src)
 
-        def w_quantise(g, n0, n1):
-            nc.vector.quantize_mx(
-                out=wc[:, g, n0:n1].bitcast(FP8X4),
-                scales=ws[:, g, n0:n1],
-                in_=wg[:, g, n0:n1, :].rearrange("p n u -> p (n u)"),
-            )
+        def w_quantise(n0, n1):
+            for g in range(2):
+                nc.vector.quantize_mx(
+                    out=wc[:, g, n0:n1].bitcast(FP8X4),
+                    scales=ws[:, g, n0:n1],
+                    in_=wg[:, g, n0:n1, :].rearrange("p n u -> p (n u)"),
+                )
 
         def gain_columns():
             gp = ps_t.tile([P, P], BF16, name="gp", tag="tb")
             nc.tensor.transpose(out=gp[:], in_=gt[:], identity=idb[:])
             nc.vector.tensor_copy(out=g32[:], in_=gp[:, 0:8])
 
-        done = set()
-        for kind, n, e in PROLOGUE:
-            done.add((kind, n))
-            if kind == "A":
-                sum_squares(n)
-            elif kind == "R":
-                root(n)
-            elif kind == "I":
-                invert(n)
-            elif kind == "C":
-                scale_rows(n, e)
-            elif kind == "T":
-                transposes(n)
-            elif kind == "D":
-                gain_and_group(n)
-            elif kind == "WT":
-                w_transposes(n)
-            elif kind == "WC":
-                w_group(n, e)
-            elif kind == "WQ":
-                for g in range(2):
-                    w_quantise(g, (0, 512)[n], (512, NOUT)[n])
-            elif kind == "GP":
-                gain_columns()
-            else:
-                assert False, kind
+        sum_squares(0)
+        root(0, 1)
+        invert(0, 1)
+        gain_columns()
+        scale_rows(0, "v")
+        transposes(0)
+        sum_squares(1)
+        root(1, 2)
+        invert(1, 2)
+        scale_rows(1, "v")
+        transposes(1)
+        sum_squares(2)
+        sum_squares(3)
+        root(2, 4)
+        w_transposes(0)
+        w_transposes(1)
+        w_group(0, "s")
+        w_group(1, "s")
+        for t in range(2):
+            for g in range(2):
+                gain_and_group(t, g)
+        invert(2, 4)
+        scale_rows(2, "g")
+        scale_rows(3, "g")
+        w_transposes(2)
+        w_transposes(3)
+        w_group(2, "v")
+        w_group(3, "s")
+        w_transposes(4)
+        w_transposes(5)
+        w_group(4, "v")
+        w_group(5, "s")
+        w_quantise(0, 512)
+        w_quantise(512, NOUT)
 
-        for it in range(-LA, NT + LF):
-            a = it + LA
-            if 0 <= a < NT:
-                if ("A", a) not in done:
-                    sum_squares(a)
-                if a == groups[group_of[a]][1] - 1 and ("R", group_of[a]) not in done:
-                    root(group_of[a])
-            if 0 <= it - LF < NT:
-                results_out(it - LF)
-            if 0 <= it < NT and ("D", it) not in done:
-                gain_and_group(it)
-            c = it + LC
-            if 0 <= c < min(NT, G_FROM) and ("C", c) not in done:
-                scale_rows(c, "v")
-            if 0 <= it + 1 < NT and ("T", it + 1) not in done:
-                transposes(it + 1)
-            if it % 2 == 1 and 1 <= it < NT:
-                quantise((it - 1) // 2)
-            r = it + LI
-            if 0 <= r < NT and r == groups[group_of[r]][0]:
-                if ("I", group_of[r]) not in done:
-                    invert(group_of[r])
-                for t in range(groups[group_of[r]][0], groups[group_of[r]][1]):
-                    if t >= G_FROM and ("C", t) not in done:
-                        scale_rows(t, "g")
-            if 0 <= it - LM < NT:
-                project(it - LM)
+        for i in range(-1, NP):
+            a, b = 2 * i, 2 * i + 1
+            last = i == NP - 1
+            m = i - 1
+            ahead = i + PA
+            if 0 <= m < NP - 1:
+                project(2 * m)
+                project(2 * m + 1)
+            if 2 <= ahead < NP:
+                sum_squares(2 * ahead)
+            if 1 <= i < NP:
+                gain_and_group(a, 0)
+                gain_and_group(a, 1)
+                gain_and_group(b, 0)
+                if not last:
+                    gain_and_group(b, 1)
+            if 0 <= m < NP - 1:
+                results_out(2 * m, "v" if 2 * m < FB_V_UNTIL else "s")
+            if 2 <= ahead < NP:
+                sum_squares(2 * ahead + 1)
+            if 0 <= m < NP - 1:
+                results_out(2 * m + 1, "v" if 2 * m < FB_V_UNTIL else "s")
+            if 2 <= ahead < NP:
+                root(2 * ahead, 2 * ahead + 2)
+            if last:
+                quantise(i, 0, 2)
+                project(a)
+                gain_and_group(b, 1)
+                quantise(i, 2, 4)
+                project(b)
+                results_out(a, "s")
+                results_out(b, "v")
+            elif 0 <= i < NP:
+                quantise(i, 0, 4)
+            if 2 <= i + PI < NP:
+                invert(2 * (i + PI), 2 * (i + PI) + 2)
+                scale_rows(2 * (i + PI), "g")
+                scale_rows(2 * (i + PI) + 1, "g")
+            if 0 <= i < NP - 1:
+                transposes(a + 2)
+                transposes(b + 2)

@@ -58,13 +58,12 @@ def tile_transformerblock_pa_t_kernel(tc, x, norm1_w, qkv_w, out_0, out_1, out_2
         ctx.enter_context(tc.manual_schedule())
 
         idf = const.tile([P, P], F32, name="idf")
-        idb = const.tile([P, P], BF16, name="idb")
-        gt = const.tile([P, P], BF16, name="gt")
+        gt = const.tile([P, 2 * P], BF16, name="gt")
         g32 = const.tile([P, 8], F32, name="g32")
         epst = const.tile([P, 1], F32, name="epst")
         warm = const.tile([P, 1], F32, name="warm")
         wsb = const.tile([P, 6, D], BF16, name="wsb")
-        wg = const.tile([P, 2, NOUT, 4], BF16, name="wg", align_bytes=64)
+        wg = const.tile([P, 2, NOUT, 2], F32, name="wg", align_bytes=64)
         wc = const.tile([P, 2, NOUT], U32, name="wc", align_bytes=64)
         ws = const.tile([P, 2, NOUT], U8, name="ws", align_bytes=64)
         xt = [const.tile([P, j1 - j0, D], BF16, name="xt%d" % li) for li, (b, j0, j1) in enumerate(loads)]
@@ -74,9 +73,8 @@ def tile_transformerblock_pa_t_kernel(tc, x, norm1_w, qkv_w, out_0, out_1, out_2
 
         nc.vector.memset(gt[:], 0.0)
         nc.vector.memset(epst[:], EPS)
-        make_identity(nc, idb[:])
         make_identity(nc, idf[:])
-        nc.scalar.dma_start(out=gt[0:8, :], in_=norm1_w.rearrange("(r c) -> r c", c=P))
+        nc.scalar.dma_start(out=gt[0:4, :], in_=norm1_w.rearrange("(r c) -> r c", c=2 * P))
 
         def load_x(li):
             b, j0, j1 = loads[li]
@@ -129,10 +127,12 @@ def tile_transformerblock_pa_t_kernel(tc, x, norm1_w, qkv_w, out_0, out_1, out_2
             xs = xsp.tile([P, D], F32, name="xs")
             xs_of[t] = xs
             r = rs[t // 2][:, t % 2 : t % 2 + 1]
+            src = x_of(t).rearrange("q (c p e) -> q c e p", c=4, e=2)
+            dst = xs[:].rearrange("q (c e p) -> q c e p", c=4, e=2)
             if engine == "g":
-                nc.gpsimd.tensor_scalar(out=xs[:], in0=x_of(t), scalar1=r, scalar2=1.0, op0=ALU.mult, op1=ALU.mult)
+                nc.gpsimd.tensor_scalar(out=dst, in0=src, scalar1=r, scalar2=1.0, op0=ALU.mult, op1=ALU.mult)
             else:
-                nc.vector.tensor_scalar(out=xs[:], in0=x_of(t), scalar1=r, scalar2=None, op0=ALU.mult)
+                nc.vector.tensor_scalar(out=dst, in0=src, scalar1=r, scalar2=None, op0=ALU.mult)
 
         def transposes(t):
             xs = xs_of[t]
@@ -208,10 +208,11 @@ def tile_transformerblock_pa_t_kernel(tc, x, norm1_w, qkv_w, out_0, out_1, out_2
 
         def w_transposes(a):
             pool = ps_a if a % 4 < 2 else ps_b
-            wp = pool.tile([P, 8, P], BF16, name="wp", tag="oa" if a % 4 < 2 else "ob")
+            wp = pool.tile([P, 4, P], F32, name="wp", tag="oa" if a % 4 < 2 else "ob")
             wp_of[a] = wp
-            for c in range(8):
-                nc.tensor.transpose(out=wp[:, c, :], in_=wsb[:, a, c * P : (c + 1) * P], identity=idb[:])
+            words = wsb[:, a, :].bitcast(F32)
+            for c in range(4):
+                nc.tensor.transpose(out=wp[:, c, :], in_=words[:, c * P : (c + 1) * P], identity=idf[:])
 
         def w_group(a, engine):
             dst = wg[:, :, a * P : (a + 1) * P, :]
@@ -226,13 +227,13 @@ def tile_transformerblock_pa_t_kernel(tc, x, norm1_w, qkv_w, out_0, out_1, out_2
                 nc.vector.quantize_mx(
                     out=wc[:, g, n0:n1].bitcast(FP8X4),
                     scales=ws[:, g, n0:n1],
-                    in_=wg[:, g, n0:n1, :].rearrange("p n u -> p (n u)"),
+                    in_=wg[:, g, n0:n1, :].rearrange("p n u -> p (n u)").bitcast(BF16),
                 )
 
         def gain_columns():
-            gp = ps_t.tile([P, P], BF16, name="gp", tag="tb")
-            nc.tensor.transpose(out=gp[:], in_=gt[:], identity=idb[:])
-            nc.vector.tensor_copy(out=g32[:], in_=gp[:, 0:8])
+            gp = ps_t.tile([P, P], F32, name="gp", tag="tb")
+            nc.tensor.transpose(out=gp[:], in_=gt[:].bitcast(F32), identity=idf[:])
+            nc.vector.tensor_copy(out=g32[:], in_=gp[:].bitcast(BF16)[:, 0:8])
 
         sum_squares(0)
         root(0, 1)
@@ -250,22 +251,22 @@ def tile_transformerblock_pa_t_kernel(tc, x, norm1_w, qkv_w, out_0, out_1, out_2
         root(2, 4)
         w_transposes(0)
         w_transposes(1)
-        w_group(0, "s")
-        w_group(1, "s")
         for t in range(2):
             for g in range(2):
                 gain_and_group(t, g)
         invert(2, 4)
         scale_rows(2, "g")
         scale_rows(3, "g")
+        w_group(0, "s")
+        w_group(1, "v")
         w_transposes(2)
         w_transposes(3)
-        w_group(2, "v")
-        w_group(3, "s")
+        w_group(2, "s")
+        w_group(3, "v")
         w_transposes(4)
         w_transposes(5)
-        w_group(4, "v")
-        w_group(5, "s")
+        w_group(4, "s")
+        w_group(5, "v")
         w_quantise(0, 512)
         w_quantise(512, NOUT)
 

@@ -302,12 +302,12 @@ def tile_transformerblock_pa_t_kernel(tc, x, norm1_w, qkv_w, out_0, out_1, out_2
                 project(b)
                 results_out(a, "s")
                 results_out(b, "v")
-            elif 0 <= i < NP:
-                quantise(i, 0, 4)
             if 2 <= i + PI < NP:
                 invert(2 * (i + PI), 2 * (i + PI) + 2)
                 scale_rows(2 * (i + PI), "g")
                 scale_rows(2 * (i + PI) + 1, "g")
+            if 0 <= i < NP - 1:
+                quantise(i, 0, 4)
             if 0 <= i < NP - 1:
                 transposes(a + 2)
                 transposes(b + 2)

@@ -62,6 +62,7 @@ def tile_transformerblock_pa_t_kernel(tc, x, norm1_w, qkv_w, out_0, out_1, out_2
         g32 = const.tile([P, 8], F32, name="g32")
         epst = const.tile([P, 1], F32, name="epst")
         warm = const.tile([P, 1], F32, name="warm")
+        zb = const.tile([P, 512], BF16, name="zb")
         wsb = const.tile([P, 6, D], BF16, name="wsb")
         wg = const.tile([P, 2, NOUT, 2], F32, name="wg", align_bytes=64)
         wc = const.tile([P, 2, NOUT], U32, name="wc", align_bytes=64)
@@ -71,6 +72,7 @@ def tile_transformerblock_pa_t_kernel(tc, x, norm1_w, qkv_w, out_0, out_1, out_2
         sq = [const.tile([P, 2], F32, name="sq%d" % i) for i in range(NP)]
         rs = [const.tile([P, 2], F32, name="rs%d" % i) for i in range(NP)]
 
+        nc.vector.memset(zb[:], 0.0)
         nc.vector.memset(gt[:], 0.0)
         nc.vector.memset(epst[:], EPS)
         make_identity(nc, idf[:])
@@ -95,6 +97,10 @@ def tile_transformerblock_pa_t_kernel(tc, x, norm1_w, qkv_w, out_0, out_1, out_2
             load_x(li)
 
         nc.scalar.activation(out=warm[:], in_=epst[:], func=ACT.Sqrt)
+
+        def keep_clock(bank, n):
+            for k in range(n):
+                nc.tensor.matmul(out=bank, lhsT=zb[:, 0:P], rhs=zb[:], start=True, stop=True)
 
         def x_of(t):
             li = load_of[t]
@@ -134,11 +140,13 @@ def tile_transformerblock_pa_t_kernel(tc, x, norm1_w, qkv_w, out_0, out_1, out_2
             else:
                 nc.vector.tensor_scalar(out=dst, in0=src, scalar1=r, scalar2=None, op0=ALU.mult)
 
-        def transposes(t):
+        def transposes(t, n_warm=0):
             xs = xs_of[t]
             banks = []
             for g in range(2):
                 tb = ps_t.tile([P, 4, P], F32, name="tb")
+                if g == 0:
+                    keep_clock(tb[:].rearrange("p u r -> p (u r)"), n_warm)
                 for u in range(4):
                     c = 4 * g + u
                     nc.tensor.transpose(out=tb[:, u, :], in_=xs[:, c * P : (c + 1) * P], identity=idf[:])
@@ -167,9 +175,10 @@ def tile_transformerblock_pa_t_kernel(tc, x, norm1_w, qkv_w, out_0, out_1, out_2
                 in_=gr_of[i][:, s0:s1, :, :].rearrange("p s r u -> p (s r u)"),
             )
 
-        def project(t):
+        def project(t, n_warm=0):
             cd, sc = cd_of[t // 2]
             oa = ps_a.tile([P, 512], F32, name="oa")
+            keep_clock(oa[:], n_warm)
             ob = ps_b.tile([P, 256], F32, name="ob")
             o_of[t] = (oa, ob)
             for o, n0, n1 in ((oa, 0, 512), (ob, 512, NOUT)):
@@ -206,10 +215,11 @@ def tile_transformerblock_pa_t_kernel(tc, x, norm1_w, qkv_w, out_0, out_1, out_2
 
         wp_of = {}
 
-        def w_transposes(a):
+        def w_transposes(a, n_warm=0):
             pool = ps_a if a % 4 < 2 else ps_b
             wp = pool.tile([P, 4, P], F32, name="wp", tag="oa" if a % 4 < 2 else "ob")
             wp_of[a] = wp
+            keep_clock(wp[:].rearrange("p u r -> p (u r)"), n_warm)
             words = wsb[:, a, :].bitcast(F32)
             for c in range(4):
                 nc.tensor.transpose(out=wp[:, c, :], in_=words[:, c * P : (c + 1) * P], identity=idf[:])
@@ -231,25 +241,26 @@ def tile_transformerblock_pa_t_kernel(tc, x, norm1_w, qkv_w, out_0, out_1, out_2
                 )
 
         def gain_columns():
-            gp = ps_t.tile([P, P], F32, name="gp", tag="tb")
-            nc.tensor.transpose(out=gp[:], in_=gt[:].bitcast(F32), identity=idf[:])
-            nc.vector.tensor_copy(out=g32[:], in_=gp[:].bitcast(BF16)[:, 0:8])
+            gp = ps_t.tile([P, 4 * P], F32, name="gp", tag="tb")
+            keep_clock(gp[:], 10)
+            nc.tensor.transpose(out=gp[:, 0:P], in_=gt[:].bitcast(F32), identity=idf[:])
+            nc.vector.tensor_copy(out=g32[:], in_=gp[:, 0:P].bitcast(BF16)[:, 0:8])
 
         sum_squares(0)
         root(0, 1)
         invert(0, 1)
         gain_columns()
         scale_rows(0, "v")
-        transposes(0)
+        transposes(0, 1)
         sum_squares(1)
         root(1, 2)
         invert(1, 2)
         scale_rows(1, "v")
-        transposes(1)
+        transposes(1, 1)
         sum_squares(2)
         sum_squares(3)
         root(2, 4)
-        w_transposes(0)
+        w_transposes(0, 1)
         w_transposes(1)
         for t in range(2):
             for g in range(2):
@@ -259,11 +270,11 @@ def tile_transformerblock_pa_t_kernel(tc, x, norm1_w, qkv_w, out_0, out_1, out_2
         scale_rows(3, "g")
         w_group(0, "s")
         w_group(1, "v")
-        w_transposes(2)
+        w_transposes(2, 1)
         w_transposes(3)
         w_group(2, "s")
         w_group(3, "v")
-        w_transposes(4)
+        w_transposes(4, 1)
         w_transposes(5)
         w_group(4, "s")
         w_group(5, "v")
@@ -276,7 +287,7 @@ def tile_transformerblock_pa_t_kernel(tc, x, norm1_w, qkv_w, out_0, out_1, out_2
             m = i - 1
             ahead = i + PA
             if 0 <= m < NP - 1:
-                project(2 * m)
+                project(2 * m, 2 if m == 0 else 0)
                 project(2 * m + 1)
             if 2 <= ahead < NP:
                 sum_squares(2 * ahead)
@@ -309,5 +320,5 @@ def tile_transformerblock_pa_t_kernel(tc, x, norm1_w, qkv_w, out_0, out_1, out_2
             if 0 <= i < NP - 1:
                 quantise(i, 0, 4)
             if 0 <= i < NP - 1:
-                transposes(a + 2)
-                transposes(b + 2)
+                transposes(a + 2, 2 if i == 0 else 0)
+                transposes(b + 2, 2 if i == 0 else 0)

@@ -55,14 +55,12 @@ def tile_transformerblock_pa_t_kernel(tc, x, norm1_w, qkv_w, out_0, out_1, out_2
         ps_t = ctx.enter_context(tc.psum_pool(name="ps_t", bufs=4))
         ps_a = ctx.enter_context(tc.psum_pool(name="ps_a", bufs=2))
         ps_b = ctx.enter_context(tc.psum_pool(name="ps_b", bufs=2))
-        ctx.enter_context(tc.manual_schedule())
 
         idf = const.tile([P, P], F32, name="idf")
         gt = const.tile([P, 2 * P], BF16, name="gt")
         g32 = const.tile([P, 8], F32, name="g32")
         epst = const.tile([P, 1], F32, name="epst")
         warm = const.tile([P, 1], F32, name="warm")
-        zb = const.tile([P, 512], BF16, name="zb")
         wsb = const.tile([P, 6, D], BF16, name="wsb")
         wg = const.tile([P, 2, NOUT, 2], F32, name="wg", align_bytes=64)
         wc = const.tile([P, 2, NOUT], U32, name="wc", align_bytes=64)
@@ -72,7 +70,6 @@ def tile_transformerblock_pa_t_kernel(tc, x, norm1_w, qkv_w, out_0, out_1, out_2
         sq = [const.tile([P, 2], F32, name="sq%d" % i) for i in range(NP)]
         rs = [const.tile([P, 2], F32, name="rs%d" % i) for i in range(NP)]
 
-        nc.vector.memset(zb[:], 0.0)
         nc.vector.memset(gt[:], 0.0)
         nc.vector.memset(epst[:], EPS)
         make_identity(nc, idf[:])
@@ -97,10 +94,6 @@ def tile_transformerblock_pa_t_kernel(tc, x, norm1_w, qkv_w, out_0, out_1, out_2
             load_x(li)
 
         nc.scalar.activation(out=warm[:], in_=epst[:], func=ACT.Sqrt)
-
-        def keep_clock(bank, n):
-            for k in range(n):
-                nc.tensor.matmul(out=bank, lhsT=zb[:, 0:P], rhs=zb[:], start=True, stop=True)
 
         def x_of(t):
             li = load_of[t]
@@ -140,13 +133,11 @@ def tile_transformerblock_pa_t_kernel(tc, x, norm1_w, qkv_w, out_0, out_1, out_2
             else:
                 nc.vector.tensor_scalar(out=dst, in0=src, scalar1=r, scalar2=None, op0=ALU.mult)
 
-        def transposes(t, n_warm=0):
+        def transposes(t):
             xs = xs_of[t]
             banks = []
             for g in range(2):
                 tb = ps_t.tile([P, 4, P], F32, name="tb")
-                if g == 0:
-                    keep_clock(tb[:].rearrange("p u r -> p (u r)"), n_warm)
                 for u in range(4):
                     c = 4 * g + u
                     nc.tensor.transpose(out=tb[:, u, :], in_=xs[:, c * P : (c + 1) * P], identity=idf[:])
@@ -175,10 +166,9 @@ def tile_transformerblock_pa_t_kernel(tc, x, norm1_w, qkv_w, out_0, out_1, out_2
                 in_=gr_of[i][:, s0:s1, :, :].rearrange("p s r u -> p (s r u)"),
             )
 
-        def project(t, n_warm=0):
+        def project(t):
             cd, sc = cd_of[t // 2]
             oa = ps_a.tile([P, 512], F32, name="oa")
-            keep_clock(oa[:], n_warm)
             ob = ps_b.tile([P, 256], F32, name="ob")
             o_of[t] = (oa, ob)
             for o, n0, n1 in ((oa, 0, 512), (ob, 512, NOUT)):
@@ -215,11 +205,10 @@ def tile_transformerblock_pa_t_kernel(tc, x, norm1_w, qkv_w, out_0, out_1, out_2
 
         wp_of = {}
 
-        def w_transposes(a, n_warm=0):
+        def w_transposes(a):
             pool = ps_a if a % 4 < 2 else ps_b
             wp = pool.tile([P, 4, P], F32, name="wp", tag="oa" if a % 4 < 2 else "ob")
             wp_of[a] = wp
-            keep_clock(wp[:].rearrange("p u r -> p (u r)"), n_warm)
             words = wsb[:, a, :].bitcast(F32)
             for c in range(4):
                 nc.tensor.transpose(out=wp[:, c, :], in_=words[:, c * P : (c + 1) * P], identity=idf[:])
@@ -241,26 +230,25 @@ def tile_transformerblock_pa_t_kernel(tc, x, norm1_w, qkv_w, out_0, out_1, out_2
                 )
 
         def gain_columns():
-            gp = ps_t.tile([P, 4 * P], F32, name="gp", tag="tb")
-            keep_clock(gp[:], 10)
-            nc.tensor.transpose(out=gp[:, 0:P], in_=gt[:].bitcast(F32), identity=idf[:])
-            nc.vector.tensor_copy(out=g32[:], in_=gp[:, 0:P].bitcast(BF16)[:, 0:8])
+            gp = ps_t.tile([P, P], F32, name="gp", tag="tb")
+            nc.tensor.transpose(out=gp[:], in_=gt[:].bitcast(F32), identity=idf[:])
+            nc.vector.tensor_copy(out=g32[:], in_=gp[:].bitcast(BF16)[:, 0:8])
 
         sum_squares(0)
         root(0, 1)
         invert(0, 1)
         gain_columns()
         scale_rows(0, "v")
-        transposes(0, 1)
+        transposes(0)
         sum_squares(1)
         root(1, 2)
         invert(1, 2)
         scale_rows(1, "v")
-        transposes(1, 1)
+        transposes(1)
         sum_squares(2)
         sum_squares(3)
         root(2, 4)
-        w_transposes(0, 1)
+        w_transposes(0)
         w_transposes(1)
         for t in range(2):
             for g in range(2):
@@ -270,11 +258,11 @@ def tile_transformerblock_pa_t_kernel(tc, x, norm1_w, qkv_w, out_0, out_1, out_2
         scale_rows(3, "g")
         w_group(0, "s")
         w_group(1, "v")
-        w_transposes(2, 1)
+        w_transposes(2)
         w_transposes(3)
         w_group(2, "s")
         w_group(3, "v")
-        w_transposes(4, 1)
+        w_transposes(4)
         w_transposes(5)
         w_group(4, "s")
         w_group(5, "v")
@@ -287,7 +275,7 @@ def tile_transformerblock_pa_t_kernel(tc, x, norm1_w, qkv_w, out_0, out_1, out_2
             m = i - 1
             ahead = i + PA
             if 0 <= m < NP - 1:
-                project(2 * m, 2 if m == 0 else 0)
+                project(2 * m)
                 project(2 * m + 1)
             if 2 <= ahead < NP:
                 sum_squares(2 * ahead)
@@ -320,5 +308,5 @@ def tile_transformerblock_pa_t_kernel(tc, x, norm1_w, qkv_w, out_0, out_1, out_2
             if 0 <= i < NP - 1:
                 quantise(i, 0, 4)
             if 0 <= i < NP - 1:
-                transposes(a + 2, 2 if i == 0 else 0)
-                transposes(b + 2, 2 if i == 0 else 0)
+                transposes(a + 2)
+                transposes(b + 2)

@@ -19,12 +19,13 @@ NOUT = 768
 JB = L // P
 NT = NB * JB
 NP = NT // 2
+NW = NOUT // P
+WIDE = 512
 EPS = 1e-6
 FLOPS = 2 * NB * L * D * NOUT
 
-PA = 3
-PI = 2
-FB_V_UNTIL = 24
+SQUARES_AHEAD = 3
+SCALING_AHEAD = 2
 
 
 def tile_transformerblock_pa_t_kernel(tc, x, norm1_w, qkv_w, out_0, out_1, out_2):
@@ -55,13 +56,14 @@ def tile_transformerblock_pa_t_kernel(tc, x, norm1_w, qkv_w, out_0, out_1, out_2
         ps_t = ctx.enter_context(tc.psum_pool(name="ps_t", bufs=4))
         ps_a = ctx.enter_context(tc.psum_pool(name="ps_a", bufs=2))
         ps_b = ctx.enter_context(tc.psum_pool(name="ps_b", bufs=2))
+        ctx.enter_context(tc.manual_schedule())
 
         idf = const.tile([P, P], F32, name="idf")
         gt = const.tile([P, 2 * P], BF16, name="gt")
-        g32 = const.tile([P, 8], F32, name="g32")
+        g32 = const.tile([P, D // P], F32, name="g32")
         epst = const.tile([P, 1], F32, name="epst")
         warm = const.tile([P, 1], F32, name="warm")
-        wsb = const.tile([P, 6, D], BF16, name="wsb")
+        wsb = const.tile([P, NW, D], BF16, name="wsb")
         wg = const.tile([P, 2, NOUT, 2], F32, name="wg", align_bytes=64)
         wc = const.tile([P, 2, NOUT], U32, name="wc", align_bytes=64)
         ws = const.tile([P, 2, NOUT], U8, name="ws", align_bytes=64)
@@ -73,23 +75,23 @@ def tile_transformerblock_pa_t_kernel(tc, x, norm1_w, qkv_w, out_0, out_1, out_2
         nc.vector.memset(gt[:], 0.0)
         nc.vector.memset(epst[:], EPS)
         make_identity(nc, idf[:])
-        nc.scalar.dma_start(out=gt[0:4, :], in_=norm1_w.rearrange("(r c) -> r c", c=2 * P))
+        nc.scalar.dma_start(out=gt[0:4, :], in_=norm1_w.rearrange("(c i) -> c i", i=2 * P))
 
         def load_x(li):
             b, j0, j1 = loads[li]
-            src = xf[b * L : (b + 1) * L, :].rearrange("(p j) d -> p j d", j=JB)
+            src = xf[b * L : (b + 1) * L, :].rearrange("(p j) k -> p j k", j=JB)
             nc.sync.dma_start(out=xt[li][:], in_=src[:, j0:j1, :])
 
-        def load_w(a0, a1):
-            src = qkv_w.rearrange("(a p) k -> p a k", p=P)
-            nc.sync.dma_start(out=wsb[:, a0:a1, :], in_=src[:, a0:a1, :])
+        def load_w(w0, w1):
+            src = qkv_w.rearrange("(w p) k -> p w k", p=P)
+            nc.sync.dma_start(out=wsb[:, w0:w1, :], in_=src[:, w0:w1, :])
 
         load_x(0)
         load_x(1)
         load_x(2)
         load_w(0, 2)
         load_w(2, 4)
-        load_w(4, 6)
+        load_w(4, NW)
         for li in range(3, len(loads)):
             load_x(li)
 
@@ -108,7 +110,7 @@ def tile_transformerblock_pa_t_kernel(tc, x, norm1_w, qkv_w, out_0, out_1, out_2
         def root(t0, t1):
             i = t0 // 2
             nc.scalar.activation(
-                out=sq[i][:, t0 % 2 : t1 - 2 * i], in_=ms[i][:, t0 % 2 : t1 - 2 * i], func=ACT.Sqrt, bias=epst[:, 0:1]
+                out=sq[i][:, t0 % 2 : t1 - 2 * i], in_=ms[i][:, t0 % 2 : t1 - 2 * i], func=ACT.Sqrt, bias=EPS
             )
 
         def invert(t0, t1):
@@ -125,22 +127,22 @@ def tile_transformerblock_pa_t_kernel(tc, x, norm1_w, qkv_w, out_0, out_1, out_2
         def scale_rows(t, engine):
             xs = xsp.tile([P, D], F32, name="xs")
             xs_of[t] = xs
-            r = rs[t // 2][:, t % 2 : t % 2 + 1]
-            src = x_of(t).rearrange("q (c p e) -> q c e p", c=4, e=2)
-            dst = xs[:].rearrange("q (c e p) -> q c e p", c=4, e=2)
+            inv_rms = rs[t // 2][:, t % 2 : t % 2 + 1]
+            src = x_of(t).rearrange("r (c p e) -> r c e p", c=4, e=2)
+            dst = xs[:].rearrange("r (c e p) -> r c e p", c=4, e=2)
             if engine == "g":
-                nc.gpsimd.tensor_scalar(out=dst, in0=src, scalar1=r, scalar2=1.0, op0=ALU.mult, op1=ALU.mult)
+                nc.gpsimd.tensor_scalar(out=dst, in0=src, scalar1=inv_rms, scalar2=1.0, op0=ALU.mult, op1=ALU.mult)
             else:
-                nc.vector.tensor_scalar(out=dst, in0=src, scalar1=r, scalar2=None, op0=ALU.mult)
+                nc.vector.tensor_scalar(out=dst, in0=src, scalar1=inv_rms, scalar2=None, op0=ALU.mult)
 
         def transposes(t):
             xs = xs_of[t]
             banks = []
             for g in range(2):
                 tb = ps_t.tile([P, 4, P], F32, name="tb")
-                for u in range(4):
-                    c = 4 * g + u
-                    nc.tensor.transpose(out=tb[:, u, :], in_=xs[:, c * P : (c + 1) * P], identity=idf[:])
+                for v in range(4):
+                    first = (4 * g + v) * P
+                    nc.tensor.transpose(out=tb[:, v, :], in_=xs[:, first : first + P], identity=idf[:])
                 banks.append(tb)
             tb_of[t] = banks
 
@@ -149,7 +151,7 @@ def tile_transformerblock_pa_t_kernel(tc, x, norm1_w, qkv_w, out_0, out_1, out_2
                 gr_of[t // 2] = grp.tile([P, 4, P, 4], BF16, name="gr", align_bytes=64)
             nc.vector.tensor_tensor(
                 out=gr_of[t // 2][:, 2 * (t % 2) + g, :, :],
-                in0=tb_of[t][g][:].rearrange("p u r -> p r u"),
+                in0=tb_of[t][g][:].rearrange("p v r -> p r v"),
                 in1=g32[:, 4 * g : 4 * g + 4].unsqueeze(1).to_broadcast([P, P, 4]),
                 op=ALU.mult,
             )
@@ -163,19 +165,22 @@ def tile_transformerblock_pa_t_kernel(tc, x, norm1_w, qkv_w, out_0, out_1, out_2
             nc.vector.quantize_mx(
                 out=cd[:, s0:s1, :].rearrange("p s r -> p (s r)").bitcast(FP8X4),
                 scales=sc[:, s0:s1, :].rearrange("p s r -> p (s r)"),
-                in_=gr_of[i][:, s0:s1, :, :].rearrange("p s r u -> p (s r u)"),
+                in_=gr_of[i][:, s0:s1, :, :].rearrange("p s r v -> p (s r v)"),
             )
 
         def project(t):
             cd, sc = cd_of[t // 2]
-            oa = ps_a.tile([P, 512], F32, name="oa")
-            ob = ps_b.tile([P, 256], F32, name="ob")
+            oa = ps_a.tile([P, WIDE], F32, name="oa")
+            if t % 2 == 0 or t // 2 == NP - 1:
+                ob = ps_b.tile([P, 2, NOUT - WIDE], F32, name="ob")
+            else:
+                ob = o_of[t - 1][1]
             o_of[t] = (oa, ob)
-            for o, n0, n1 in ((oa, 0, 512), (ob, 512, NOUT)):
+            for bank, n0, n1 in ((oa[:], 0, WIDE), (ob[:, t % 2, :], WIDE, NOUT)):
                 for g in range(2):
                     s = 2 * (t % 2) + g
                     nc.tensor.matmul_mx(
-                        out=o[:],
+                        out=bank,
                         lhsT=cd[:, s, :].bitcast(FP8X4),
                         lhsT_scale=sc[:, s, :],
                         rhs=wc[:, g, n0:n1].bitcast(FP8X4),
@@ -189,33 +194,41 @@ def tile_transformerblock_pa_t_kernel(tc, x, norm1_w, qkv_w, out_0, out_1, out_2
             b, j0, j1 = stores[si]
             j = t % JB
             if j == j0:
-                os_of[si] = osp.tile([P, 6, j1 - j0, P], F32, name="osb")
+                os_of[si] = osp.tile([P, NW, j1 - j0, P], F32, name="osb")
             osb = os_of[si]
             oa, ob = o_of[t]
-            nc.scalar.copy(out=osb[:, 0:4, j - j0, :], in_=oa[:].rearrange("p (c f) -> p c f", c=4))
-            if engine_b == "v":
-                nc.vector.tensor_copy(out=osb[:, 4:6, j - j0, :], in_=ob[:].rearrange("p (c f) -> p c f", c=2))
-            else:
-                nc.scalar.copy(out=osb[:, 4:6, j - j0, :], in_=ob[:].rearrange("p (c f) -> p c f", c=2))
+            n_wide = WIDE // P
+            nc.scalar.copy(out=osb[:, 0:n_wide, j - j0, :], in_=oa[:].rearrange("p (o f) -> p o f", o=n_wide))
+            if t // 2 == NP - 1 or t % 2 == 1:
+                if t // 2 == NP - 1:
+                    narrow_dst = osb[:, n_wide:NW, j - j0, :]
+                    narrow_src = ob[:, t % 2, :].rearrange("p (o f) -> p o f", o=NW - n_wide)
+                else:
+                    narrow_dst = osb[:, n_wide:NW, j - 1 - j0 : j + 1 - j0, :]
+                    narrow_src = ob[:].rearrange("p c (o f) -> p o c f", o=NW - n_wide)
+                if engine_b == "v":
+                    nc.vector.tensor_copy(out=narrow_dst, in_=narrow_src)
+                else:
+                    nc.scalar.copy(out=narrow_dst, in_=narrow_src)
             if j == j1 - 1:
-                for i in range(3):
-                    dst = outs[i].rearrange("b n l f -> (b n) l f")[2 * b : 2 * b + 2, :, :]
-                    dst = dst.rearrange("n (p j) f -> p n j f", j=JB)
-                    nc.sync.dma_start(out=dst[:, :, j0:j1, :], in_=osb[:, 2 * i : 2 * i + 2, :, :])
+                for qkv in range(3):
+                    dst = outs[qkv].rearrange("b a l f -> (b a) l f")[2 * b : 2 * b + 2, :, :]
+                    dst = dst.rearrange("a (p j) f -> p a j f", j=JB)
+                    nc.sync.dma_start(out=dst[:, :, j0:j1, :], in_=osb[:, 2 * qkv : 2 * qkv + 2, :, :])
 
         wp_of = {}
 
-        def w_transposes(a):
-            pool = ps_a if a % 4 < 2 else ps_b
-            wp = pool.tile([P, 4, P], F32, name="wp", tag="oa" if a % 4 < 2 else "ob")
-            wp_of[a] = wp
-            words = wsb[:, a, :].bitcast(F32)
+        def w_transposes(w):
+            pool = ps_a if w % 4 < 2 else ps_b
+            wp = pool.tile([P, 4, P], F32, name="wp", tag="oa" if w % 4 < 2 else "ob")
+            wp_of[w] = wp
+            pairs = wsb[:, w, :].bitcast(F32)
             for c in range(4):
-                nc.tensor.transpose(out=wp[:, c, :], in_=words[:, c * P : (c + 1) * P], identity=idf[:])
+                nc.tensor.transpose(out=wp[:, c, :], in_=pairs[:, c * P : (c + 1) * P], identity=idf[:])
 
-        def w_group(a, engine):
-            dst = wg[:, :, a * P : (a + 1) * P, :]
-            src = wp_of[a][:].rearrange("p (g u) n -> p g n u", g=2)
+        def w_group(w, engine):
+            dst = wg[:, :, w * P : (w + 1) * P, :]
+            src = wp_of[w][:].rearrange("p (g u) n -> p g n u", g=2)
             if engine == "v":
                 nc.vector.tensor_copy(out=dst, in_=src)
             else:
@@ -232,7 +245,7 @@ def tile_transformerblock_pa_t_kernel(tc, x, norm1_w, qkv_w, out_0, out_1, out_2
         def gain_columns():
             gp = ps_t.tile([P, P], F32, name="gp", tag="tb")
             nc.tensor.transpose(out=gp[:], in_=gt[:].bitcast(F32), identity=idf[:])
-            nc.vector.tensor_copy(out=g32[:], in_=gp[:].bitcast(BF16)[:, 0:8])
+            nc.vector.tensor_copy(out=g32[:], in_=gp[:].bitcast(BF16)[:, 0 : D // P])
 
         sum_squares(0)
         root(0, 1)
@@ -266,47 +279,48 @@ def tile_transformerblock_pa_t_kernel(tc, x, norm1_w, qkv_w, out_0, out_1, out_2
         w_transposes(5)
         w_group(4, "s")
         w_group(5, "v")
-        w_quantise(0, 512)
-        w_quantise(512, NOUT)
+        w_quantise(0, WIDE)
+        w_quantise(WIDE, NOUT)
 
         for i in range(-1, NP):
-            a, b = 2 * i, 2 * i + 1
+            t_even, t_odd = 2 * i, 2 * i + 1
             last = i == NP - 1
             m = i - 1
-            ahead = i + PA
-            if 0 <= m < NP - 1:
+            ahead = i + SQUARES_AHEAD
+            narrow = "v" if ahead < NP else "s"
+            if 0 <= m:
                 project(2 * m)
                 project(2 * m + 1)
             if 2 <= ahead < NP:
                 sum_squares(2 * ahead)
-            if 1 <= i < NP:
-                gain_and_group(a, 0)
-                gain_and_group(a, 1)
-                gain_and_group(b, 0)
+            if 1 <= i:
+                gain_and_group(t_even, 0)
+                gain_and_group(t_even, 1)
+                gain_and_group(t_odd, 0)
                 if not last:
-                    gain_and_group(b, 1)
-            if 0 <= m < NP - 1:
-                results_out(2 * m, "v" if 2 * m < FB_V_UNTIL else "s")
+                    gain_and_group(t_odd, 1)
+            scaled = i + SCALING_AHEAD
+            if 2 <= scaled < NP:
+                invert(2 * scaled, 2 * scaled + 2)
+                scale_rows(2 * scaled, "g")
+                scale_rows(2 * scaled + 1, "g")
+            if 0 <= m:
+                results_out(2 * m, narrow)
             if 2 <= ahead < NP:
                 sum_squares(2 * ahead + 1)
-            if 0 <= m < NP - 1:
-                results_out(2 * m + 1, "v" if 2 * m < FB_V_UNTIL else "s")
+            if 0 <= m:
+                results_out(2 * m + 1, narrow)
             if 2 <= ahead < NP:
                 root(2 * ahead, 2 * ahead + 2)
             if last:
                 quantise(i, 0, 2)
-                project(a)
-                gain_and_group(b, 1)
+                project(t_even)
+                gain_and_group(t_odd, 1)
                 quantise(i, 2, 4)
-                project(b)
-                results_out(a, "s")
-                results_out(b, "v")
-            if 2 <= i + PI < NP:
-                invert(2 * (i + PI), 2 * (i + PI) + 2)
-                scale_rows(2 * (i + PI), "g")
-                scale_rows(2 * (i + PI) + 1, "g")
-            if 0 <= i < NP - 1:
+                project(t_odd)
+                results_out(t_even, "s")
+                results_out(t_odd, "v")
+            if 0 <= i and not last:
                 quantise(i, 0, 4)
-            if 0 <= i < NP - 1:
-                transposes(a + 2)
-                transposes(b + 2)
+                transposes(t_even + 2)
+                transposes(t_odd + 2)

from contextlib import ExitStack

import concourse.mybir as mybir
from concourse.masks import make_identity

BF16 = mybir.dt.bfloat16
F32 = mybir.dt.float32
U32 = mybir.dt.uint32
U8 = mybir.dt.uint8
FP8X4 = mybir.dt.float8_e4m3fn_x4
ACT = mybir.ActivationFunctionType
ALU = mybir.AluOpType

P = 128
NB = 4
L = 1024
D = 1024
NOUT = 768
JB = L // P
NT = NB * JB
NP = NT // 2
NW = NOUT // P
WIDE = 512
EPS = 1e-6
FLOPS = 2 * NB * L * D * NOUT

SQUARES_AHEAD = 3
SCALING_AHEAD = 2


def tile_transformerblock_pa_t_kernel(tc, x, norm1_w, qkv_w, out_0, out_1, out_2):
    nc = tc.nc
    outs = (out_0, out_1, out_2)
    xf = x.flatten_outer_dims()

    loads = [(0, 0, 1), (0, 1, 2), (0, 2, 4), (0, 4, 8)]
    loads += [(b, j, j + 4) for b in range(1, NB) for j in (0, 4)]
    stores = [(b, j, j + 4) for b in range(NB - 1) for j in (0, 4)]
    stores += [(NB - 1, 0, 2), (NB - 1, 2, 4), (NB - 1, 4, 6), (NB - 1, 6, 7), (NB - 1, 7, 8)]
    load_of = {}
    for li, (b, j0, j1) in enumerate(loads):
        for j in range(j0, j1):
            load_of[b * JB + j] = li
    store_of = {}
    for si, (b, j0, j1) in enumerate(stores):
        for j in range(j0, j1):
            store_of[b * JB + j] = si

    with ExitStack() as ctx:
        const = ctx.enter_context(tc.tile_pool(name="const", bufs=1))
        xsp = ctx.enter_context(tc.tile_pool(name="xsp", bufs=8))
        grp = ctx.enter_context(tc.tile_pool(name="grp", bufs=3))
        cdp = ctx.enter_context(tc.tile_pool(name="cdp", bufs=3))
        jkp = ctx.enter_context(tc.tile_pool(name="jkp", bufs=2))
        osp = ctx.enter_context(tc.tile_pool(name="osp", bufs=4))
        ps_t = ctx.enter_context(tc.psum_pool(name="ps_t", bufs=4))
        ps_a = ctx.enter_context(tc.psum_pool(name="ps_a", bufs=2))
        ps_b = ctx.enter_context(tc.psum_pool(name="ps_b", bufs=2))
        ctx.enter_context(tc.manual_schedule())

        idf = const.tile([P, P], F32, name="idf")
        gt = const.tile([P, 2 * P], BF16, name="gt")
        g32 = const.tile([P, D // P], F32, name="g32")
        epst = const.tile([P, 1], F32, name="epst")
        warm = const.tile([P, 1], F32, name="warm")
        wsb = const.tile([P, NW, D], BF16, name="wsb")
        wg = const.tile([P, 2, NOUT, 2], F32, name="wg", align_bytes=64)
        wc = const.tile([P, 2, NOUT], U32, name="wc", align_bytes=64)
        ws = const.tile([P, 2, NOUT], U8, name="ws", align_bytes=64)
        xt = [const.tile([P, j1 - j0, D], BF16, name="xt%d" % li) for li, (b, j0, j1) in enumerate(loads)]
        ms = [const.tile([P, 2], F32, name="ms%d" % i) for i in range(NP)]
        sq = [const.tile([P, 2], F32, name="sq%d" % i) for i in range(NP)]
        rs = [const.tile([P, 2], F32, name="rs%d" % i) for i in range(NP)]

        nc.vector.memset(gt[:], 0.0)
        nc.vector.memset(epst[:], EPS)
        make_identity(nc, idf[:])
        nc.scalar.dma_start(out=gt[0:4, :], in_=norm1_w.rearrange("(c i) -> c i", i=2 * P))

        def load_x(li):
            b, j0, j1 = loads[li]
            src = xf[b * L : (b + 1) * L, :].rearrange("(p j) k -> p j k", j=JB)
            nc.sync.dma_start(out=xt[li][:], in_=src[:, j0:j1, :])

        def load_w(w0, w1):
            src = qkv_w.rearrange("(w p) k -> p w k", p=P)
            nc.sync.dma_start(out=wsb[:, w0:w1, :], in_=src[:, w0:w1, :])

        load_x(0)
        load_x(1)
        load_x(2)
        load_w(0, 2)
        load_w(2, 4)
        load_w(4, NW)
        for li in range(3, len(loads)):
            load_x(li)

        nc.scalar.activation(out=warm[:], in_=epst[:], func=ACT.Sqrt)

        def x_of(t):
            li = load_of[t]
            return xt[li][:, t % JB - loads[li][1], :]

        def sum_squares(t):
            junk = jkp.tile([P, D], BF16, name="junk")
            nc.scalar.activation(
                out=junk[:], in_=x_of(t), func=ACT.Square, scale=1.0 / 32.0, accum_out=ms[t // 2][:, t % 2 : t % 2 + 1]
            )

        def root(t0, t1):
            i = t0 // 2
            nc.scalar.activation(
                out=sq[i][:, t0 % 2 : t1 - 2 * i], in_=ms[i][:, t0 % 2 : t1 - 2 * i], func=ACT.Sqrt, bias=EPS
            )

        def invert(t0, t1):
            i = t0 // 2
            nc.vector.reciprocal(out=rs[i][:, t0 % 2 : t1 - 2 * i], in_=sq[i][:, t0 % 2 : t1 - 2 * i])

        xs_of = {}
        tb_of = {}
        gr_of = {}
        cd_of = {}
        o_of = {}
        os_of = {}

        def scale_rows(t, engine):
            xs = xsp.tile([P, D], F32, name="xs")
            xs_of[t] = xs
            inv_rms = rs[t // 2][:, t % 2 : t % 2 + 1]
            src = x_of(t).rearrange("r (c p e) -> r c e p", c=4, e=2)
            dst = xs[:].rearrange("r (c e p) -> r c e p", c=4, e=2)
            if engine == "g":
                nc.gpsimd.tensor_scalar(out=dst, in0=src, scalar1=inv_rms, scalar2=1.0, op0=ALU.mult, op1=ALU.mult)
            else:
                nc.vector.tensor_scalar(out=dst, in0=src, scalar1=inv_rms, scalar2=None, op0=ALU.mult)

        def transposes(t):
            xs = xs_of[t]
            banks = []
            for g in range(2):
                tb = ps_t.tile([P, 4, P], F32, name="tb")
                for v in range(4):
                    first = (4 * g + v) * P
                    nc.tensor.transpose(out=tb[:, v, :], in_=xs[:, first : first + P], identity=idf[:])
                banks.append(tb)
            tb_of[t] = banks

        def gain_and_group(t, g):
            if t % 2 == 0 and g == 0:
                gr_of[t // 2] = grp.tile([P, 4, P, 4], BF16, name="gr", align_bytes=64)
            nc.vector.tensor_tensor(
                out=gr_of[t // 2][:, 2 * (t % 2) + g, :, :],
                in0=tb_of[t][g][:].rearrange("p v r -> p r v"),
                in1=g32[:, 4 * g : 4 * g + 4].unsqueeze(1).to_broadcast([P, P, 4]),
                op=ALU.mult,
            )

        def quantise(i, s0, s1):
            if s0 == 0:
                cd = cdp.tile([P, 4, P], U32, name="cd", align_bytes=64)
                sc = cdp.tile([P, 4, P], U8, name="sc", align_bytes=64)
                cd_of[i] = (cd, sc)
            cd, sc = cd_of[i]
            nc.vector.quantize_mx(
                out=cd[:, s0:s1, :].rearrange("p s r -> p (s r)").bitcast(FP8X4),
                scales=sc[:, s0:s1, :].rearrange("p s r -> p (s r)"),
                in_=gr_of[i][:, s0:s1, :, :].rearrange("p s r v -> p (s r v)"),
            )

        def project(t):
            cd, sc = cd_of[t // 2]
            oa = ps_a.tile([P, WIDE], F32, name="oa")
            if t % 2 == 0 or t // 2 == NP - 1:
                ob = ps_b.tile([P, 2, NOUT - WIDE], F32, name="ob")
            else:
                ob = o_of[t - 1][1]
            o_of[t] = (oa, ob)
            for bank, n0, n1 in ((oa[:], 0, WIDE), (ob[:, t % 2, :], WIDE, NOUT)):
                for g in range(2):
                    s = 2 * (t % 2) + g
                    nc.tensor.matmul_mx(
                        out=bank,
                        lhsT=cd[:, s, :].bitcast(FP8X4),
                        lhsT_scale=sc[:, s, :],
                        rhs=wc[:, g, n0:n1].bitcast(FP8X4),
                        rhs_scale=ws[:, g, n0:n1],
                        start=(g == 0),
                        stop=(g == 1),
                    )

        def results_out(t, engine_b):
            si = store_of[t]
            b, j0, j1 = stores[si]
            j = t % JB
            if j == j0:
                os_of[si] = osp.tile([P, NW, j1 - j0, P], F32, name="osb")
            osb = os_of[si]
            oa, ob = o_of[t]
            n_wide = WIDE // P
            nc.scalar.copy(out=osb[:, 0:n_wide, j - j0, :], in_=oa[:].rearrange("p (o f) -> p o f", o=n_wide))
            if t // 2 == NP - 1 or t % 2 == 1:
                if t // 2 == NP - 1:
                    narrow_dst = osb[:, n_wide:NW, j - j0, :]
                    narrow_src = ob[:, t % 2, :].rearrange("p (o f) -> p o f", o=NW - n_wide)
                else:
                    narrow_dst = osb[:, n_wide:NW, j - 1 - j0 : j + 1 - j0, :]
                    narrow_src = ob[:].rearrange("p c (o f) -> p o c f", o=NW - n_wide)
                if engine_b == "v":
                    nc.vector.tensor_copy(out=narrow_dst, in_=narrow_src)
                else:
                    nc.scalar.copy(out=narrow_dst, in_=narrow_src)
            if j == j1 - 1:
                for qkv in range(3):
                    dst = outs[qkv].rearrange("b a l f -> (b a) l f")[2 * b : 2 * b + 2, :, :]
                    dst = dst.rearrange("a (p j) f -> p a j f", j=JB)
                    nc.sync.dma_start(out=dst[:, :, j0:j1, :], in_=osb[:, 2 * qkv : 2 * qkv + 2, :, :])

        wp_of = {}

        def w_transposes(w):
            pool = ps_a if w % 4 < 2 else ps_b
            wp = pool.tile([P, 4, P], F32, name="wp", tag="oa" if w % 4 < 2 else "ob")
            wp_of[w] = wp
            pairs = wsb[:, w, :].bitcast(F32)
            for c in range(4):
                nc.tensor.transpose(out=wp[:, c, :], in_=pairs[:, c * P : (c + 1) * P], identity=idf[:])

        def w_group(w, engine):
            dst = wg[:, :, w * P : (w + 1) * P, :]
            src = wp_of[w][:].rearrange("p (g u) n -> p g n u", g=2)
            if engine == "v":
                nc.vector.tensor_copy(out=dst, in_=src)
            else:
                nc.scalar.copy(out=dst, in_=src)

        def w_quantise(n0, n1):
            for g in range(2):
                nc.vector.quantize_mx(
                    out=wc[:, g, n0:n1].bitcast(FP8X4),
                    scales=ws[:, g, n0:n1],
                    in_=wg[:, g, n0:n1, :].rearrange("p n u -> p (n u)").bitcast(BF16),
                )

        def gain_columns():
            gp = ps_t.tile([P, P], F32, name="gp", tag="tb")
            nc.tensor.transpose(out=gp[:], in_=gt[:].bitcast(F32), identity=idf[:])
            nc.vector.tensor_copy(out=g32[:], in_=gp[:].bitcast(BF16)[:, 0 : D // P])

        sum_squares(0)
        root(0, 1)
        invert(0, 1)
        gain_columns()
        scale_rows(0, "v")
        transposes(0)
        sum_squares(1)
        root(1, 2)
        invert(1, 2)
        scale_rows(1, "v")
        transposes(1)
        sum_squares(2)
        sum_squares(3)
        root(2, 4)
        w_transposes(0)
        w_transposes(1)
        for t in range(2):
            for g in range(2):
                gain_and_group(t, g)
        invert(2, 4)
        scale_rows(2, "g")
        scale_rows(3, "g")
        w_group(0, "s")
        w_group(1, "v")
        w_transposes(2)
        w_transposes(3)
        w_group(2, "s")
        w_group(3, "v")
        w_transposes(4)
        w_transposes(5)
        w_group(4, "s")
        w_group(5, "v")
        w_quantise(0, WIDE)
        w_quantise(WIDE, NOUT)

        for i in range(-1, NP):
            t_even, t_odd = 2 * i, 2 * i + 1
            last = i == NP - 1
            m = i - 1
            ahead = i + SQUARES_AHEAD
            narrow = "v" if ahead < NP else "s"
            if 0 <= m:
                project(2 * m)
                project(2 * m + 1)
            if 2 <= ahead < NP:
                sum_squares(2 * ahead)
            if 1 <= i:
                gain_and_group(t_even, 0)
                gain_and_group(t_even, 1)
                gain_and_group(t_odd, 0)
                if not last:
                    gain_and_group(t_odd, 1)
            scaled = i + SCALING_AHEAD
            if 2 <= scaled < NP:
                invert(2 * scaled, 2 * scaled + 2)
                scale_rows(2 * scaled, "g")
                scale_rows(2 * scaled + 1, "g")
            if 0 <= m:
                results_out(2 * m, narrow)
            if 2 <= ahead < NP:
                sum_squares(2 * ahead + 1)
            if 0 <= m:
                results_out(2 * m + 1, narrow)
            if 2 <= ahead < NP:
                root(2 * ahead, 2 * ahead + 2)
            if last:
                quantise(i, 0, 2)
                project(t_even)
                gain_and_group(t_odd, 1)
                quantise(i, 2, 4)
                project(t_odd)
                results_out(t_even, "s")
                results_out(t_odd, "v")
            if 0 <= i and not last:
                quantise(i, 0, 4)
                transposes(t_even + 2)
                transposes(t_odd + 2)
